import numpy as np
import ml_dtypes


def mxq(x, axis, fmt="e4m3"):
    dtype, down = {"e4m3": (ml_dtypes.float8_e4m3fn, 7), "e5m2": (ml_dtypes.float8_e5m2, 14)}[fmt]
    v = np.moveaxis(np.asarray(x, np.float32).astype(ml_dtypes.bfloat16).astype(np.float64), axis, -1)
    blocks = v.reshape(v.shape[:-1] + (-1, 32))
    amax = np.abs(blocks).max(-1, keepdims=True)
    byte = np.maximum(np.where(amax > 0, np.frexp(amax)[1] - 1 + 127, 0) - down, 1)
    scale = np.exp2(byte - 127.0)
    codes = (blocks / scale).astype(np.float32).astype(dtype).astype(np.float64)
    return np.moveaxis((codes * scale).reshape(v.shape), -1, axis)


WIDE = False


def mx_kscale(k):
    if not WIDE:
        return np.ones(k)
    levels = np.array([10, -10, 5, -5, 0])
    a = np.random.permutation(np.resize(levels, k // 512 * 4)).reshape(k // 512, 4)
    idx = np.arange(k)
    return np.exp2(a[idx // 512, idx % 128 // 32])


BF16 = ml_dtypes.bfloat16


def bf(x):
    return np.asarray(x, np.float32).astype(BF16)


def f64(x):
    return np.asarray(x).astype(np.float64)


B, N, D, M = 4, 1024, 512, 1024


def setup_inputs():
    s = mx_kscale(D)
    return {"x": bf(np.random.standard_normal((B, N, D)) * s), "mem": bf(np.random.standard_normal((1, D, M)) * 2.0 / s[None, :, None])}


def reference(x, mem):
    xf = f64(x)
    d = xf.shape[-1]
    m = f64(mem)[0]
    logits = (mxq(m, 0, "e4m3").T @ mxq(xf, 2, "e4m3").transpose(0, 2, 1)) / np.sqrt(float(d))
    e = np.exp(logits - logits.max(axis=1, keepdims=True))
    return (mxq(e, 1, "e4m3").transpose(0, 2, 1) @ mxq(m, 1, "e4m3").T) / e.sum(axis=1)[:, :, None]

@@ -1,0 +1,309 @@
+from contextlib import ExitStack
+
+import concourse.mybir as mybir
+from concourse.masks import make_identity
+
+F32 = mybir.dt.float32
+BF16 = mybir.dt.bfloat16
+U32 = mybir.dt.uint32
+U8 = mybir.dt.uint8
+FP8X4 = mybir.dt.float8_e4m3fn_x4
+ACT = mybir.ActivationFunctionType
+ALU = mybir.AluOpType
+AX = mybir.AxisListType
+
+P = 128
+D = 512
+M = 1024
+TOK = 4096
+NG = 8
+NT = 32
+SCALE = 1.0 / (512.0 ** 0.5)
+FLOPS = 2 * 2 * TOK * M * D
+PINNED = True
+XA = 5
+
+
+def tile_p4transformerda7_kernel(tc, x, mem, out):
+    nc = tc.nc
+    xf = x.flatten_outer_dims()
+    mf = mem.flatten_outer_dims()
+    of = out.flatten_outer_dims()
+
+    with ExitStack() as ctx:
+        const = ctx.enter_context(tc.tile_pool(name="const", bufs=1))
+        work = ctx.enter_context(tc.tile_pool(name="work", bufs=3))
+        small = ctx.enter_context(tc.tile_pool(name="small", bufs=6))
+        psum = ctx.enter_context(tc.psum_pool(name="psum", bufs=1))
+        if PINNED:
+            ctx.enter_context(tc.manual_schedule())
+
+        mraw = const.tile([P, 4 * M], BF16, name="mraw")
+        mraw_k = mraw[:].rearrange("q (k c) -> q k c", k=4)
+        xs = []
+
+        def load_x(g):
+            xg = const.tile([P, 4 * D], BF16, name="xs%d" % g)
+            nc.sync.dma_start(
+                out=xg[:].rearrange("r (i d) -> r i d", i=4),
+                in_=xf[512 * g : 512 * g + 512, :].rearrange("(r i) d -> r i d", i=4),
+            )
+            xs.append(xg)
+
+        load_x(0)
+        for u in range(2):
+            nc.sync.dma_start(
+                out=mraw_k[:, 2 * u : 2 * u + 2, :],
+                in_=mf[256 * u : 256 * u + 256, :].rearrange("(p e) c -> p e c", e=2),
+            )
+        for g in range(1, NG):
+            load_x(g)
+
+        warm = const.tile([P, 1], F32, name="warm")
+        nc.vector.memset(warm[:], 0.0)
+        warm2 = const.tile([P, 1], F32, name="warm2")
+        nc.scalar.activation(out=warm2[:], in_=warm[:], func=ACT.Exp)
+        ident_f = const.tile([P, P], F32, name="ident_f")
+        make_identity(nc, ident_f[:])
+        ident_b = const.tile([P, P], BF16, name="ident_b")
+        make_identity(nc, ident_b[:])
+
+        st = {}
+
+        def copy_on(eng, dst, src):
+            if eng == "v":
+                nc.vector.tensor_copy(out=dst, in_=src)
+            else:
+                nc.scalar.copy(out=dst, in_=src)
+
+        def x_transpose(g, h):
+            xw = xs[g][:].bitcast(F32)
+            tx = psum.tile([P, 2, 2, P], F32, name="tx", tag="T", bufs=3)
+            for i2 in range(2):
+                for u in range(2):
+                    col = (2 * h + i2) * 256 + 128 * u
+                    nc.tensor.transpose(tx[:, i2, u, :], xw[:, col : col + 128], ident_f[:])
+            st["tx%d_%d" % (g, h)] = tx
+
+        def x_copy(g, h, eng):
+            if h == 0:
+                gx = work.tile([P, 1024], F32, name="gx", align_bytes=64)
+                st["gx%d" % g] = gx
+            gx_v = st["gx%d" % g][:].rearrange("q (i r u) -> q i r u", i=4, r=P, u=2)
+            tx = st["tx%d_%d" % (g, h)]
+            copy_on(eng, gx_v[:, 2 * h : 2 * h + 2], tx[:].rearrange("q i u r -> q i r u"))
+
+        def x_quantise(g):
+            q = const.tile([P, 512], U32, name="xq%d" % g, align_bytes=64)
+            s = const.tile([P, 512], U8, name="xsc%d" % g, align_bytes=64)
+            nc.vector.quantize_mx(
+                out=q[:].bitcast(FP8X4), scales=s[:], in_=st["gx%d" % g][:].bitcast(BF16)
+            )
+            st["xq%d" % g] = q
+            st["xsc%d" % g] = s
+
+        g1 = const.tile([P, 4 * M], BF16, name="g1", align_bytes=64)
+        m1q = const.tile([P, M], U32, name="m1q", align_bytes=64)
+        m1s = const.tile([P, M], U8, name="m1s", align_bytes=64)
+        g1_v = g1[:].rearrange("q (c t p k) -> q c t p k", c=2, t=4, p=P, k=4)
+        mraw_v = mraw[:].rearrange("q (k c p t) -> q c t p k", k=4, c=2, p=P, t=4)
+
+        def m1_quantise(c):
+            nc.vector.quantize_mx(
+                out=m1q[:, 512 * c : 512 * c + 512].bitcast(FP8X4),
+                scales=m1s[:, 512 * c : 512 * c + 512],
+                in_=g1[:, 2048 * c : 2048 * c + 2048],
+            )
+
+        m2q = const.tile([P, 2 * D], U32, name="m2q", align_bytes=64)
+        m2s = const.tile([P, 2 * D], U8, name="m2s", align_bytes=64)
+        mw = mraw[:].bitcast(F32).rearrange("q (k w) -> q k w", k=4)
+        g2 = const.tile([P, 2 * D * 2], F32, name="g2", align_bytes=64)
+        g2_v = g2[:].rearrange("q (c u a e v) -> q c u a e v", c=2, u=2, a=P, e=2, v=2)
+
+        def m2_transpose(c, u):
+            tm = psum.tile([P, 2, 2, P], F32, name="tm", tag="T", bufs=3)
+            for e in range(2):
+                for v in range(2):
+                    nc.tensor.transpose(
+                        tm[:, e, v, :], mw[:, 2 * u + e, 256 * c + v : 256 * c + 256 : 2], ident_f[:]
+                    )
+            st["tm%d%d" % (c, u)] = tm
+
+        def m2_copy(c, u, eng):
+            copy_on(eng, g2_v[:, c, u], st["tm%d%d" % (c, u)][:].rearrange("q e v a -> q a e v"))
+
+        def m2_quantise(c):
+            nc.vector.quantize_mx(
+                out=m2q[:, 512 * c : 512 * c + 512].bitcast(FP8X4),
+                scales=m2s[:, 512 * c : 512 * c + 512],
+                in_=g2[:].bitcast(BF16)[:, 2048 * c : 2048 * c + 2048],
+            )
+
+        def logits(n):
+            g, i = divmod(n, 4)
+            cols = slice(128 * i, 128 * i + 128)
+            for c in range(2):
+                lg = psum.tile([P, 512], F32, name="lg", tag="L", bufs=4)
+                nc.tensor.matmul_mx(
+                    out=lg[:],
+                    lhsT=st["xq%d" % g][:, cols].bitcast(FP8X4),
+                    lhsT_scale=st["xsc%d" % g][:, cols],
+                    rhs=m1q[:, 512 * c : 512 * c + 512].bitcast(FP8X4),
+                    rhs_scale=m1s[:, 512 * c : 512 * c + 512],
+                    start=True,
+                    stop=True,
+                )
+                st["lg%d_%d" % (n, c)] = lg
+
+        def row_max(n):
+            mx = small.tile([P, 2], F32, name="mx")
+            for c in range(2):
+                nc.vector.reduce_max(out=mx[:, c : c + 1], in_=st["lg%d_%d" % (n, c)][:], axis=AX.X)
+            st["mx%d" % n] = mx
+
+        def neg_bias(n):
+            mx = st["mx%d" % n]
+            nb = small.tile([P, 1], F32, name="nb")
+            nc.vector.tensor_scalar(
+                out=nb[:], in0=mx[:, 0:1], scalar1=mx[:, 1:2], scalar2=-SCALE, op0=ALU.max, op1=ALU.mult
+            )
+            st["nb%d" % n] = nb
+
+        def exps(n):
+            if n % 2 == 0:
+                ss = small.tile([P, 2, 2], F32, name="ss")
+                st["ss%d" % (n // 2)] = ss
+            ss = st["ss%d" % (n // 2)]
+            e = work.tile([P, M], BF16, name="e")
+            for c in range(2):
+                nc.scalar.activation(
+                    out=e[:, 512 * c : 512 * c + 512],
+                    in_=st["lg%d_%d" % (n, c)][:],
+                    func=ACT.Exp,
+                    bias=st["nb%d" % n][:],
+                    scale=SCALE,
+                    accum_out=ss[:, n % 2, c : c + 1],
+                )
+            st["e%d" % n] = e
+
+        def e_transpose(n):
+            e = st["e%d" % n]
+            for c in range(2):
+                tp = psum.tile([P, 4, P], BF16, name="tp", tag="T", bufs=3)
+                for t in range(4):
+                    k = 4 * c + t
+                    nc.tensor.transpose(tp[:, t, :], e[:, 128 * k : 128 * k + 128], ident_b[:])
+                st["tp%d_%d" % (n, c)] = tp
+
+        def e_copy(n, c, eng):
+            if ("ge%d" % n) not in st:
+                ge = work.tile([P, M], BF16, name="ge", align_bytes=64)
+                st["ge%d" % n] = ge
+            dst = st["ge%d" % n][:].rearrange("q (c r t) -> q c r t", c=2, r=P, t=4)
+            copy_on(eng, dst[:, c], st["tp%d_%d" % (n, c)][:].rearrange("q t r -> q r t"))
+
+        def e_quantise(n):
+            eq = work.tile([P, 256], U32, name="eq", align_bytes=64)
+            es = work.tile([P, 256], U8, name="es", align_bytes=64)
+            nc.vector.quantize_mx(out=eq[:].bitcast(FP8X4), scales=es[:], in_=st["ge%d" % n][:])
+            st["eq%d" % n] = eq
+            st["es%d" % n] = es
+
+        def pair_sums(pr):
+            tot = small.tile([P, 2], F32, name="tot")
+            nc.vector.reduce_sum(out=tot[:], in_=st["ss%d" % pr][:], axis=AX.X)
+            rc = small.tile([P, 2], F32, name="rc")
+            nc.vector.reciprocal(out=rc[:], in_=tot[:])
+            st["rc%d" % pr] = rc
+
+        def out_matmul(n):
+            eq = st["eq%d" % n]
+            es = st["es%d" % n]
+            acc = psum.tile([P, D], F32, name="acc", tag="O", bufs=1)
+            for c in range(2):
+                nc.tensor.matmul_mx(
+                    out=acc[:],
+                    lhsT=eq[:, 128 * c : 128 * c + 128].bitcast(FP8X4),
+                    lhsT_scale=es[:, 128 * c : 128 * c + 128],
+                    rhs=m2q[:, 512 * c : 512 * c + 512].bitcast(FP8X4),
+                    rhs_scale=m2s[:, 512 * c : 512 * c + 512],
+                    start=(c == 0),
+                    stop=(c == 1),
+                )
+            st["acc%d" % n] = acc
+
+        def out_copy(n):
+            g, i = divmod(n, 4)
+            if n % 2 == 0:
+                ob = work.tile([P, 2, D], F32, name="ob")
+                st["ob%d" % (n // 2)] = ob
+            ob = st["ob%d" % (n // 2)]
+            rc = st["rc%d" % (n // 2)]
+            nc.scalar.activation(
+                out=ob[:, n % 2, :], in_=st["acc%d" % n][:], func=ACT.Copy, scale=rc[:, n % 2 : n % 2 + 1]
+            )
+            if n % 2 == 1:
+                dview = of[512 * g : 512 * g + 512, :].rearrange("(r i) d -> r i d", i=4)
+                nc.sync.dma_start(out=dview[:, i - 1 : i + 1, :], in_=ob[:])
+
+        x_transpose(0, 0)
+        x_transpose(0, 1)
+        x_copy(0, 0, "v")
+        x_copy(0, 1, "s")
+        x_quantise(0)
+        nc.vector.tensor_copy(out=g1_v[:, 0], in_=mraw_v[:, 0])
+        nc.scalar.copy(out=g1_v[:, 1, 0:3], in_=mraw_v[:, 1, 0:3])
+        m1_quantise(0)
+        nc.vector.tensor_copy(out=g1_v[:, 1, 3:4], in_=mraw_v[:, 1, 3:4])
+        m1_quantise(1)
+        m2_transpose(0, 0)
+        m2_transpose(0, 1)
+        m2_transpose(1, 0)
+        logits(0)
+        m2_copy(0, 0, "s")
+        m2_copy(0, 1, "s")
+        m2_copy(1, 0, "s")
+        m2_transpose(1, 1)
+        m2_copy(1, 1, "s")
+
+        def live(n):
+            return 0 <= n < NT
+
+        for step in range(-1, NT + 4):
+            if live(step - 3):
+                out_copy(step - 3)
+            if live(step - 1):
+                e_transpose(step - 1)
+            if step >= 0 and live(step + 1):
+                logits(step + 1)
+            if live(step):
+                row_max(step)
+            if live(step - 2):
+                e_quantise(step - 2)
+            for g in range(1, NG):
+                if 4 * g - XA + 3 == step:
+                    x_quantise(g)
+            if live(step):
+                neg_bias(step)
+            if step == 0:
+                m2_quantise(0)
+                m2_quantise(1)
+            if live(step - 2):
+                out_matmul(step - 2)
+            for g in range(1, NG):
+                for h in range(2):
+                    if 4 * g - XA + h == step:
+                        x_transpose(g, h)
+            if live(step - 1):
+                e_copy(step - 1, 1, "s")
+            if live(step):
+                exps(step)
+            if live(step - 1):
+                e_copy(step - 1, 0, "v")
+            if live(step - 1) and (step - 1) % 2 == 1:
+                pair_sums((step - 1) // 2)
+            for g in range(1, NG):
+                for h in range(2):
+                    if 4 * g - XA + h + 1 == step:
+                        x_copy(g, h, "vs"[h])

@@ -21,7 +21,6 @@ NT = 32
 SCALE = 1.0 / (512.0 ** 0.5)
 FLOPS = 2 * 2 * TOK * M * D
 PINNED = True
-XA = 5
 
 
 def tile_p4transformerda7_kernel(tc, x, mem, out):
@@ -78,7 +77,7 @@ def tile_p4transformerda7_kernel(tc, x, mem, out):
 
         def x_transpose(g, h):
             xw = xs[g][:].bitcast(F32)
-            tx = psum.tile([P, 2, 2, P], F32, name="tx", tag="T", bufs=3)
+            tx = psum.tile([P, 2, 2, P], F32, name="tx", tag="T", bufs=2)
             for i2 in range(2):
                 for u in range(2):
                     col = (2 * h + i2) * 256 + 128 * u
@@ -87,7 +86,7 @@ def tile_p4transformerda7_kernel(tc, x, mem, out):
 
         def x_copy(g, h, eng):
             if h == 0:
-                gx = work.tile([P, 1024], F32, name="gx", align_bytes=64)
+                gx = const.tile([P, 1024], F32, name="gx", align_bytes=64)
                 st["gx%d" % g] = gx
             gx_v = st["gx%d" % g][:].rearrange("q (i r u) -> q i r u", i=4, r=P, u=2)
             tx = st["tx%d_%d" % (g, h)]
@@ -99,8 +98,34 @@ def tile_p4transformerda7_kernel(tc, x, mem, out):
             nc.vector.quantize_mx(
                 out=q[:].bitcast(FP8X4), scales=s[:], in_=st["gx%d" % g][:].bitcast(BF16)
             )
-            st["xq%d" % g] = q
-            st["xsc%d" % g] = s
+            for i in range(4):
+                st["xc%d" % (4 * g + i)] = (q[:, 128 * i : 128 * i + 128], s[:, 128 * i : 128 * i + 128])
+
+        def x1_transpose(n):
+            g, i = divmod(n, 4)
+            xw = xs[g][:].bitcast(F32)
+            tx = psum.tile([P, 2, P], F32, name="tx1", tag="T", bufs=2)
+            for u in range(2):
+                col = i * 256 + 128 * u
+                nc.tensor.transpose(tx[:, u, :], xw[:, col : col + 128], ident_f[:])
+            st["tx1_%d" % n] = tx
+
+        def x1_copy(n, eng):
+            gx = work.tile([P, 256], F32, name="gx1", align_bytes=64)
+            copy_on(
+                eng,
+                gx[:].rearrange("q (r u) -> q r u", r=P, u=2),
+                st["tx1_%d" % n][:].rearrange("q u r -> q r u"),
+            )
+            st["gx1_%d" % n] = gx
+
+        def x1_quantise(n):
+            q = const.tile([P, P], U32, name="xq1_%d" % n, align_bytes=64)
+            s = const.tile([P, P], U8, name="xs1_%d" % n, align_bytes=64)
+            nc.vector.quantize_mx(
+                out=q[:].bitcast(FP8X4), scales=s[:], in_=st["gx1_%d" % n][:].bitcast(BF16)
+            )
+            st["xc%d" % n] = (q[:], s[:])
 
         g1 = const.tile([P, 4 * M], BF16, name="g1", align_bytes=64)
         m1q = const.tile([P, M], U32, name="m1q", align_bytes=64)
@@ -121,8 +146,8 @@ def tile_p4transformerda7_kernel(tc, x, mem, out):
         g2 = const.tile([P, 2 * D * 2], F32, name="g2", align_bytes=64)
         g2_v = g2[:].rearrange("q (c u a e v) -> q c u a e v", c=2, u=2, a=P, e=2, v=2)
 
-        def m2_transpose(c, u):
-            tm = psum.tile([P, 2, 2, P], F32, name="tm", tag="T", bufs=3)
+        def m2_transpose(c, u, tag):
+            tm = psum.tile([P, 2, 2, P], F32, name="tm", tag=tag, bufs=2)
             for e in range(2):
                 for v in range(2):
                     nc.tensor.transpose(
@@ -141,14 +166,13 @@ def tile_p4transformerda7_kernel(tc, x, mem, out):
             )
 
         def logits(n):
-            g, i = divmod(n, 4)
-            cols = slice(128 * i, 128 * i + 128)
+            codes, scales = st["xc%d" % n]
             for c in range(2):
                 lg = psum.tile([P, 512], F32, name="lg", tag="L", bufs=4)
                 nc.tensor.matmul_mx(
                     out=lg[:],
-                    lhsT=st["xq%d" % g][:, cols].bitcast(FP8X4),
-                    lhsT_scale=st["xsc%d" % g][:, cols],
+                    lhsT=codes.bitcast(FP8X4),
+                    lhsT_scale=scales,
                     rhs=m1q[:, 512 * c : 512 * c + 512].bitcast(FP8X4),
                     rhs_scale=m1s[:, 512 * c : 512 * c + 512],
                     start=True,
@@ -170,38 +194,47 @@ def tile_p4transformerda7_kernel(tc, x, mem, out):
             )
             st["nb%d" % n] = nb
 
-        def exps(n):
-            if n % 2 == 0:
+        def exp_half(n, c):
+            if n % 2 == 0 and c == 0:
                 ss = small.tile([P, 2, 2], F32, name="ss")
                 st["ss%d" % (n // 2)] = ss
             ss = st["ss%d" % (n // 2)]
-            e = work.tile([P, M], BF16, name="e")
-            for c in range(2):
-                nc.scalar.activation(
-                    out=e[:, 512 * c : 512 * c + 512],
-                    in_=st["lg%d_%d" % (n, c)][:],
-                    func=ACT.Exp,
-                    bias=st["nb%d" % n][:],
-                    scale=SCALE,
-                    accum_out=ss[:, n % 2, c : c + 1],
-                )
-            st["e%d" % n] = e
+            e = work.tile([P, 512], BF16, name="e%d" % c)
+            nc.scalar.activation(
+                out=e[:],
+                in_=st["lg%d_%d" % (n, c)][:],
+                func=ACT.Exp,
+                bias=st["nb%d" % n][:],
+                scale=SCALE,
+                accum_out=ss[:, n % 2, c : c + 1],
+            )
+            st["e%d_%d" % (n, c)] = e
 
-        def e_transpose(n):
-            e = st["e%d" % n]
-            for c in range(2):
-                tp = psum.tile([P, 4, P], BF16, name="tp", tag="T", bufs=3)
-                for t in range(4):
-                    k = 4 * c + t
-                    nc.tensor.transpose(tp[:, t, :], e[:, 128 * k : 128 * k + 128], ident_b[:])
-                st["tp%d_%d" % (n, c)] = tp
+        def e_transpose_half(n, c):
+            if c == 0:
+                tw = psum.tile([P, 8, P], BF16, name="tw", tag="T", bufs=2)
+                st["tw%d" % n] = tw
+            tw = st["tw%d" % n]
+            e = st["e%d_%d" % (n, c)]
+            for t in range(4):
+                nc.tensor.transpose(tw[:, 4 * c + t, :], e[:, 128 * t : 128 * t + 128], ident_b[:])
 
-        def e_copy(n, c, eng):
-            if ("ge%d" % n) not in st:
-                ge = work.tile([P, M], BF16, name="ge", align_bytes=64)
-                st["ge%d" % n] = ge
-            dst = st["ge%d" % n][:].rearrange("q (c r t) -> q c r t", c=2, r=P, t=4)
-            copy_on(eng, dst[:, c], st["tp%d_%d" % (n, c)][:].rearrange("q t r -> q r t"))
+        def e_copy(n):
+            s1 = work.tile([P, M], BF16, name="s1", bufs=2)
+            nc.vector.tensor_copy(out=s1[:], in_=st["tw%d" % n][:].rearrange("q k r -> q (k r)"))
+            st["s1_%d" % n] = s1
+
+        def e_regroup(n):
+            ge = work.tile([P, M], BF16, name="ge", align_bytes=64, bufs=1)
+            nc.gpsimd.tensor_scalar(
+                out=ge[:].rearrange("q (c r t) -> q c r t", c=2, r=P, t=4),
+                in0=st["s1_%d" % n][:].rearrange("q (c t r) -> q c r t", c=2, t=4, r=P),
+                scalar1=1.0,
+                scalar2=0.0,
+                op0=ALU.mult,
+                op1=ALU.add,
+            )
+            st["ge%d" % n] = ge
 
         def e_quantise(n):
             eq = work.tile([P, 256], U32, name="eq", align_bytes=64)
@@ -210,17 +243,20 @@ def tile_p4transformerda7_kernel(tc, x, mem, out):
             st["eq%d" % n] = eq
             st["es%d" % n] = es
 
-        def pair_sums(pr):
+        def pair_sum(pr):
             tot = small.tile([P, 2], F32, name="tot")
             nc.vector.reduce_sum(out=tot[:], in_=st["ss%d" % pr][:], axis=AX.X)
+            st["tot%d" % pr] = tot
+
+        def pair_recip(pr):
             rc = small.tile([P, 2], F32, name="rc")
-            nc.vector.reciprocal(out=rc[:], in_=tot[:])
+            nc.vector.reciprocal(out=rc[:], in_=st["tot%d" % pr][:])
             st["rc%d" % pr] = rc
 
         def out_matmul(n):
             eq = st["eq%d" % n]
             es = st["es%d" % n]
-            acc = psum.tile([P, D], F32, name="acc", tag="O", bufs=1)
+            acc = psum.tile([P, D], F32, name="acc", tag="O", bufs=2)
             for c in range(2):
                 nc.tensor.matmul_mx(
                     out=acc[:],
@@ -257,53 +293,52 @@ def tile_p4transformerda7_kernel(tc, x, mem, out):
         m1_quantise(0)
         nc.vector.tensor_copy(out=g1_v[:, 1, 3:4], in_=mraw_v[:, 1, 3:4])
         m1_quantise(1)
-        m2_transpose(0, 0)
-        m2_transpose(0, 1)
-        m2_transpose(1, 0)
+        m2_transpose(0, 0, "O")
+        m2_transpose(0, 1, "O")
+        m2_transpose(1, 0, "T")
+        m2_transpose(1, 1, "T")
         logits(0)
-        m2_copy(0, 0, "s")
-        m2_copy(0, 1, "s")
-        m2_copy(1, 0, "s")
-        m2_transpose(1, 1)
-        m2_copy(1, 1, "s")
+        logits(1)
+        for c in range(2):
+            for u in range(2):
+                m2_copy(c, u, "s")
 
         def live(n):
             return 0 <= n < NT
 
-        for step in range(-1, NT + 4):
-            if live(step - 3):
-                out_copy(step - 3)
-            if live(step - 1):
-                e_transpose(step - 1)
-            if step >= 0 and live(step + 1):
-                logits(step + 1)
+        for step in range(NT + 4):
             if live(step):
                 row_max(step)
-            if live(step - 2):
-                e_quantise(step - 2)
-            for g in range(1, NG):
-                if 4 * g - XA + 3 == step:
-                    x_quantise(g)
+            if step % 2 == 0 and live(step - 1):
+                pair_sum((step - 2) // 2)
+            if step % 2 == 1 and live(step - 2):
+                pair_recip((step - 3) // 2)
             if live(step):
                 neg_bias(step)
             if step == 0:
                 m2_quantise(0)
                 m2_quantise(1)
+            if live(step - 1):
+                e_copy(step - 1)
+            if live(step + 3) and step + 3 >= 4:
+                x1_quantise(step + 3)
+            if live(step - 2):
+                e_quantise(step - 2)
+            if live(step - 1):
+                e_regroup(step - 1)
+            if live(step):
+                exp_half(step, 0)
+                e_transpose_half(step, 0)
+            if live(step + 4):
+                x1_transpose(step + 4)
+            if live(step):
+                exp_half(step, 1)
+                e_transpose_half(step, 1)
+            if live(step - 3):
+                out_copy(step - 3)
+            if live(step + 4):
+                x1_copy(step + 4, "s")
             if live(step - 2):
                 out_matmul(step - 2)
-            for g in range(1, NG):
-                for h in range(2):
-                    if 4 * g - XA + h == step:
-                        x_transpose(g, h)
-            if live(step - 1):
-                e_copy(step - 1, 1, "s")
-            if live(step):
-                exps(step)
-            if live(step - 1):
-                e_copy(step - 1, 0, "v")
-            if live(step - 1) and (step - 1) % 2 == 1:
-                pair_sums((step - 1) // 2)
-            for g in range(1, NG):
-                for h in range(2):
-                    if 4 * g - XA + h + 1 == step:
-                        x_copy(g, h, "vs"[h])
+            if live(step + 2):
+                logits(step + 2)

@@ -20,7 +20,7 @@ NG = 8
 NT = 32
 SCALE = 1.0 / (512.0 ** 0.5)
 FLOPS = 2 * 2 * TOK * M * D
-PINNED = True
+BANKS = {"L": 4, "T": 2, "X": 1, "O": 1}
 
 
 def tile_p4transformerda7_kernel(tc, x, mem, out):
@@ -34,27 +34,49 @@ def tile_p4transformerda7_kernel(tc, x, mem, out):
         work = ctx.enter_context(tc.tile_pool(name="work", bufs=3))
         small = ctx.enter_context(tc.tile_pool(name="small", bufs=6))
         psum = ctx.enter_context(tc.psum_pool(name="psum", bufs=1))
-        if PINNED:
-            ctx.enter_context(tc.manual_schedule())
+        ctx.enter_context(tc.manual_schedule())
 
-        mraw = const.tile([P, 4 * M], BF16, name="mraw")
-        mraw_k = mraw[:].rearrange("q (k c) -> q k c", k=4)
-        xs = []
+        st = {}
+
+        def bank(shape, dtype, tag, name):
+            return psum.tile(shape, dtype, name=name, tag=tag, bufs=BANKS[tag])
+
+        def copy_on(eng, dst, src):
+            if eng == "v":
+                nc.vector.tensor_copy(out=dst, in_=src)
+            else:
+                nc.scalar.copy(out=dst, in_=src)
+
+        def x_rows(g):
+            return xf[512 * g : 512 * g + 512, :].rearrange("(r i) d -> r i d", i=4)
+
+        def load_x_half(h):
+            t = const.tile([P, 2 * D], BF16, name="xs0%d" % h)
+            nc.sync.dma_start(
+                out=t[:].rearrange("r (i d) -> r i d", i=2), in_=x_rows(0)[:, 2 * h : 2 * h + 2, :]
+            )
+            for i in range(2):
+                st["xw%d" % (2 * h + i)] = t[:].bitcast(F32)[:, 256 * i : 256 * i + 256]
 
         def load_x(g):
-            xg = const.tile([P, 4 * D], BF16, name="xs%d" % g)
-            nc.sync.dma_start(
-                out=xg[:].rearrange("r (i d) -> r i d", i=4),
-                in_=xf[512 * g : 512 * g + 512, :].rearrange("(r i) d -> r i d", i=4),
-            )
-            xs.append(xg)
+            t = const.tile([P, 4 * D], BF16, name="xs%d" % g)
+            nc.sync.dma_start(out=t[:].rearrange("r (i d) -> r i d", i=4), in_=x_rows(g))
+            for i in range(4):
+                st["xw%d" % (4 * g + i)] = t[:].bitcast(F32)[:, 256 * i : 256 * i + 256]
 
-        load_x(0)
-        for u in range(2):
-            nc.sync.dma_start(
-                out=mraw_k[:, 2 * u : 2 * u + 2, :],
-                in_=mf[256 * u : 256 * u + 256, :].rearrange("(p e) c -> p e c", e=2),
-            )
+        mraw = []
+        load_x_half(0)
+        for c in range(2):
+            t = const.tile([P, 4 * 512], BF16, name="mraw%d" % c)
+            for u in range(2):
+                nc.sync.dma_start(
+                    out=t[:].rearrange("q (k j) -> q k j", k=4)[:, 2 * u : 2 * u + 2, :],
+                    in_=mf[256 * u : 256 * u + 256, 512 * c : 512 * c + 512].rearrange(
+                        "(p e) j -> p e j", e=2
+                    ),
+                )
+            mraw.append(t)
+        load_x_half(1)
         for g in range(1, NG):
             load_x(g)
 
@@ -67,124 +89,88 @@ def tile_p4transformerda7_kernel(tc, x, mem, out):
         ident_b = const.tile([P, P], BF16, name="ident_b")
         make_identity(nc, ident_b[:])
 
-        st = {}
-
-        def copy_on(eng, dst, src):
-            if eng == "v":
-                nc.vector.tensor_copy(out=dst, in_=src)
-            else:
-                nc.scalar.copy(out=dst, in_=src)
-
-        def x_transpose(g, h):
-            xw = xs[g][:].bitcast(F32)
-            tx = psum.tile([P, 2, 2, P], F32, name="tx", tag="T", bufs=2)
-            for i2 in range(2):
+        def x_transpose(n, cnt, tag):
+            tx = bank([P, cnt, 2, P], F32, tag, "tx")
+            for i in range(cnt):
                 for u in range(2):
-                    col = (2 * h + i2) * 256 + 128 * u
-                    nc.tensor.transpose(tx[:, i2, u, :], xw[:, col : col + 128], ident_f[:])
-            st["tx%d_%d" % (g, h)] = tx
+                    nc.tensor.transpose(
+                        tx[:, i, u, :], st["xw%d" % (n + i)][:, 128 * u : 128 * u + 128], ident_f[:]
+                    )
+            st["tx%d" % n] = tx
 
-        def x_copy(g, h, eng):
-            if h == 0:
-                gx = const.tile([P, 1024], F32, name="gx", align_bytes=64)
-                st["gx%d" % g] = gx
-            gx_v = st["gx%d" % g][:].rearrange("q (i r u) -> q i r u", i=4, r=P, u=2)
-            tx = st["tx%d_%d" % (g, h)]
-            copy_on(eng, gx_v[:, 2 * h : 2 * h + 2], tx[:].rearrange("q i u r -> q i r u"))
-
-        def x_quantise(g):
-            q = const.tile([P, 512], U32, name="xq%d" % g, align_bytes=64)
-            s = const.tile([P, 512], U8, name="xsc%d" % g, align_bytes=64)
-            nc.vector.quantize_mx(
-                out=q[:].bitcast(FP8X4), scales=s[:], in_=st["gx%d" % g][:].bitcast(BF16)
-            )
-            for i in range(4):
-                st["xc%d" % (4 * g + i)] = (q[:, 128 * i : 128 * i + 128], s[:, 128 * i : 128 * i + 128])
-
-        def x1_transpose(n):
-            g, i = divmod(n, 4)
-            xw = xs[g][:].bitcast(F32)
-            tx = psum.tile([P, 2, P], F32, name="tx1", tag="T", bufs=2)
-            for u in range(2):
-                col = i * 256 + 128 * u
-                nc.tensor.transpose(tx[:, u, :], xw[:, col : col + 128], ident_f[:])
-            st["tx1_%d" % n] = tx
-
-        def x1_copy(n, eng):
-            gx = work.tile([P, 256], F32, name="gx1", align_bytes=64)
+        def x_copy(n, cnt, eng):
+            gx = work.tile([P, 256 * cnt], F32, name="gx%d" % cnt, align_bytes=64)
             copy_on(
                 eng,
-                gx[:].rearrange("q (r u) -> q r u", r=P, u=2),
-                st["tx1_%d" % n][:].rearrange("q u r -> q r u"),
+                gx[:].rearrange("q (i r u) -> q i r u", i=cnt, r=P, u=2),
+                st["tx%d" % n][:].rearrange("q i u r -> q i r u"),
             )
-            st["gx1_%d" % n] = gx
+            st["gx%d" % n] = gx
 
-        def x1_quantise(n):
-            q = const.tile([P, P], U32, name="xq1_%d" % n, align_bytes=64)
-            s = const.tile([P, P], U8, name="xs1_%d" % n, align_bytes=64)
-            nc.vector.quantize_mx(
-                out=q[:].bitcast(FP8X4), scales=s[:], in_=st["gx1_%d" % n][:].bitcast(BF16)
-            )
-            st["xc%d" % n] = (q[:], s[:])
+        def x_quantise(n, cnt):
+            q = const.tile([P, P * cnt], U32, name="xq%d" % n, align_bytes=64)
+            s = const.tile([P, P * cnt], U8, name="xsc%d" % n, align_bytes=64)
+            nc.vector.quantize_mx(out=q[:].bitcast(FP8X4), scales=s[:], in_=st["gx%d" % n][:].bitcast(BF16))
+            for i in range(cnt):
+                st["xc%d" % (n + i)] = (q[:, 128 * i : 128 * i + 128], s[:, 128 * i : 128 * i + 128])
 
-        g1 = const.tile([P, 4 * M], BF16, name="g1", align_bytes=64)
-        m1q = const.tile([P, M], U32, name="m1q", align_bytes=64)
-        m1s = const.tile([P, M], U8, name="m1s", align_bytes=64)
-        g1_v = g1[:].rearrange("q (c t p k) -> q c t p k", c=2, t=4, p=P, k=4)
-        mraw_v = mraw[:].rearrange("q (k c p t) -> q c t p k", k=4, c=2, p=P, t=4)
+        def m1_regroup(c, eng, t0, t1):
+            if ("g1_%d" % c) not in st:
+                g1 = const.tile([P, 2048], BF16, name="g1_%d" % c, align_bytes=64)
+                st["g1_%d" % c] = g1
+            dst = st["g1_%d" % c][:].rearrange("q (t p k) -> q t p k", t=4, p=P, k=4)
+            src = mraw[c][:].rearrange("q (k p t) -> q t p k", k=4, p=P, t=4)
+            copy_on(eng, dst[:, t0:t1], src[:, t0:t1])
 
         def m1_quantise(c):
-            nc.vector.quantize_mx(
-                out=m1q[:, 512 * c : 512 * c + 512].bitcast(FP8X4),
-                scales=m1s[:, 512 * c : 512 * c + 512],
-                in_=g1[:, 2048 * c : 2048 * c + 2048],
-            )
-
-        m2q = const.tile([P, 2 * D], U32, name="m2q", align_bytes=64)
-        m2s = const.tile([P, 2 * D], U8, name="m2s", align_bytes=64)
-        mw = mraw[:].bitcast(F32).rearrange("q (k w) -> q k w", k=4)
-        g2 = const.tile([P, 2 * D * 2], F32, name="g2", align_bytes=64)
-        g2_v = g2[:].rearrange("q (c u a e v) -> q c u a e v", c=2, u=2, a=P, e=2, v=2)
+            q = const.tile([P, 512], U32, name="m1q%d" % c, align_bytes=64)
+            s = const.tile([P, 512], U8, name="m1s%d" % c, align_bytes=64)
+            nc.vector.quantize_mx(out=q[:].bitcast(FP8X4), scales=s[:], in_=st["g1_%d" % c][:])
+            st["m1_%d" % c] = (q, s)
 
         def m2_transpose(c, u, tag):
-            tm = psum.tile([P, 2, 2, P], F32, name="tm", tag=tag, bufs=2)
+            mw = mraw[c][:].bitcast(F32).rearrange("q (k w) -> q k w", k=4)
+            tm = bank([P, 2, 2, P], F32, tag, "tm")
             for e in range(2):
                 for v in range(2):
-                    nc.tensor.transpose(
-                        tm[:, e, v, :], mw[:, 2 * u + e, 256 * c + v : 256 * c + 256 : 2], ident_f[:]
-                    )
+                    nc.tensor.transpose(tm[:, e, v, :], mw[:, 2 * u + e, v : 256 : 2], ident_f[:])
             st["tm%d%d" % (c, u)] = tm
 
         def m2_copy(c, u, eng):
-            copy_on(eng, g2_v[:, c, u], st["tm%d%d" % (c, u)][:].rearrange("q e v a -> q a e v"))
+            if ("g2_%d" % c) not in st:
+                g2 = const.tile([P, 1024], F32, name="g2_%d" % c, align_bytes=64)
+                st["g2_%d" % c] = g2
+            dst = st["g2_%d" % c][:].rearrange("q (u a e v) -> q u a e v", u=2, a=P, e=2, v=2)
+            copy_on(eng, dst[:, u], st["tm%d%d" % (c, u)][:].rearrange("q e v a -> q a e v"))
 
         def m2_quantise(c):
-            nc.vector.quantize_mx(
-                out=m2q[:, 512 * c : 512 * c + 512].bitcast(FP8X4),
-                scales=m2s[:, 512 * c : 512 * c + 512],
-                in_=g2[:].bitcast(BF16)[:, 2048 * c : 2048 * c + 2048],
-            )
+            q = const.tile([P, 512], U32, name="m2q%d" % c, align_bytes=64)
+            s = const.tile([P, 512], U8, name="m2s%d" % c, align_bytes=64)
+            nc.vector.quantize_mx(out=q[:].bitcast(FP8X4), scales=s[:], in_=st["g2_%d" % c][:].bitcast(BF16))
+            st["m2_%d" % c] = (q, s)
 
-        def logits(n):
+        def logits(n, c):
             codes, scales = st["xc%d" % n]
-            for c in range(2):
-                lg = psum.tile([P, 512], F32, name="lg", tag="L", bufs=4)
-                nc.tensor.matmul_mx(
-                    out=lg[:],
-                    lhsT=codes.bitcast(FP8X4),
-                    lhsT_scale=scales,
-                    rhs=m1q[:, 512 * c : 512 * c + 512].bitcast(FP8X4),
-                    rhs_scale=m1s[:, 512 * c : 512 * c + 512],
-                    start=True,
-                    stop=True,
-                )
-                st["lg%d_%d" % (n, c)] = lg
+            q, s = st["m1_%d" % c]
+            lg = bank([P, 512], F32, "L", "lg")
+            nc.tensor.matmul_mx(
+                out=lg[:],
+                lhsT=codes.bitcast(FP8X4),
+                lhsT_scale=scales,
+                rhs=q[:].bitcast(FP8X4),
+                rhs_scale=s[:],
+                start=True,
+                stop=True,
+            )
+            st["lg%d_%d" % (n, c)] = lg
 
-        def row_max(n):
-            mx = small.tile([P, 2], F32, name="mx")
-            for c in range(2):
-                nc.vector.reduce_max(out=mx[:, c : c + 1], in_=st["lg%d_%d" % (n, c)][:], axis=AX.X)
-            st["mx%d" % n] = mx
+        def row_max(n, c):
+            if c == 0:
+                mx = small.tile([P, 2], F32, name="mx")
+                st["mx%d" % n] = mx
+            nc.vector.reduce_max(
+                out=st["mx%d" % n][:, c : c + 1], in_=st["lg%d_%d" % (n, c)][:], axis=AX.X
+            )
 
         def neg_bias(n):
             mx = st["mx%d" % n]
@@ -210,14 +196,24 @@ def tile_p4transformerda7_kernel(tc, x, mem, out):
             )
             st["e%d_%d" % (n, c)] = e
 
+        def short_way(n):
+            return n >= NT - 2
+
         def e_transpose_half(n, c):
-            if c == 0:
-                tw = psum.tile([P, 8, P], BF16, name="tw", tag="T", bufs=2)
-                st["tw%d" % n] = tw
-            tw = st["tw%d" % n]
             e = st["e%d_%d" % (n, c)]
+            if short_way(n):
+                td = bank([P, 4, P], BF16, "L", "td")
+                st["td%d_%d" % (n, c)] = td
+                dst = td
+                k0 = 0
+            else:
+                if c == 0:
+                    tw = bank([P, 8, P], BF16, "T", "tw")
+                    st["tw%d" % n] = tw
+                dst = st["tw%d" % n]
+                k0 = 4 * c
             for t in range(4):
-                nc.tensor.transpose(tw[:, 4 * c + t, :], e[:, 128 * t : 128 * t + 128], ident_b[:])
+                nc.tensor.transpose(dst[:, k0 + t, :], e[:, 128 * t : 128 * t + 128], ident_b[:])
 
         def e_copy(n):
             s1 = work.tile([P, M], BF16, name="s1", bufs=2)
@@ -225,7 +221,7 @@ def tile_p4transformerda7_kernel(tc, x, mem, out):
             st["s1_%d" % n] = s1
 
         def e_regroup(n):
-            ge = work.tile([P, M], BF16, name="ge", align_bytes=64, bufs=1)
+            ge = work.tile([P, M], BF16, name="ge", align_bytes=64, bufs=2)
             nc.gpsimd.tensor_scalar(
                 out=ge[:].rearrange("q (c r t) -> q c r t", c=2, r=P, t=4),
                 in0=st["s1_%d" % n][:].rearrange("q (c t r) -> q c r t", c=2, t=4, r=P),
@@ -236,9 +232,16 @@ def tile_p4transformerda7_kernel(tc, x, mem, out):
             )
             st["ge%d" % n] = ge
 
+        def e_copy_short(n, c, eng):
+            if ("ge%d" % n) not in st:
+                ge = work.tile([P, M], BF16, name="ged", align_bytes=64, bufs=2)
+                st["ge%d" % n] = ge
+            dst = st["ge%d" % n][:].rearrange("q (c r t) -> q c r t", c=2, r=P, t=4)
+            copy_on(eng, dst[:, c], st["td%d_%d" % (n, c)][:].rearrange("q t r -> q r t"))
+
         def e_quantise(n):
-            eq = work.tile([P, 256], U32, name="eq", align_bytes=64)
-            es = work.tile([P, 256], U8, name="es", align_bytes=64)
+            eq = work.tile([P, 256], U32, name="eq", align_bytes=64, bufs=4)
+            es = work.tile([P, 256], U8, name="es", align_bytes=64, bufs=4)
             nc.vector.quantize_mx(out=eq[:].bitcast(FP8X4), scales=es[:], in_=st["ge%d" % n][:])
             st["eq%d" % n] = eq
             st["es%d" % n] = es
@@ -253,92 +256,139 @@ def tile_p4transformerda7_kernel(tc, x, mem, out):
             nc.vector.reciprocal(out=rc[:], in_=st["tot%d" % pr][:])
             st["rc%d" % pr] = rc
 
-        def out_matmul(n):
+        def out_matmul(n, tag):
             eq = st["eq%d" % n]
             es = st["es%d" % n]
-            acc = psum.tile([P, D], F32, name="acc", tag="O", bufs=2)
+            acc = bank([P, D], F32, tag, "acc")
             for c in range(2):
+                q, s = st["m2_%d" % c]
                 nc.tensor.matmul_mx(
                     out=acc[:],
                     lhsT=eq[:, 128 * c : 128 * c + 128].bitcast(FP8X4),
                     lhsT_scale=es[:, 128 * c : 128 * c + 128],
-                    rhs=m2q[:, 512 * c : 512 * c + 512].bitcast(FP8X4),
-                    rhs_scale=m2s[:, 512 * c : 512 * c + 512],
+                    rhs=q[:].bitcast(FP8X4),
+                    rhs_scale=s[:],
                     start=(c == 0),
                     stop=(c == 1),
                 )
             st["acc%d" % n] = acc
 
-        def out_copy(n):
-            g, i = divmod(n, 4)
+        def out_copy(n, eng):
             if n % 2 == 0:
                 ob = work.tile([P, 2, D], F32, name="ob")
                 st["ob%d" % (n // 2)] = ob
             ob = st["ob%d" % (n // 2)]
-            rc = st["rc%d" % (n // 2)]
-            nc.scalar.activation(
-                out=ob[:, n % 2, :], in_=st["acc%d" % n][:], func=ACT.Copy, scale=rc[:, n % 2 : n % 2 + 1]
-            )
-            if n % 2 == 1:
-                dview = of[512 * g : 512 * g + 512, :].rearrange("(r i) d -> r i d", i=4)
-                nc.sync.dma_start(out=dview[:, i - 1 : i + 1, :], in_=ob[:])
+            rc = st["rc%d" % (n // 2)][:, n % 2 : n % 2 + 1]
+            if eng == "v":
+                nc.vector.tensor_scalar(
+                    out=ob[:, n % 2, :], in0=st["acc%d" % n][:], scalar1=rc, scalar2=None, op0=ALU.mult
+                )
+            else:
+                nc.scalar.activation(out=ob[:, n % 2, :], in_=st["acc%d" % n][:], func=ACT.Copy, scale=rc)
 
-        x_transpose(0, 0)
-        x_transpose(0, 1)
-        x_copy(0, 0, "v")
-        x_copy(0, 1, "s")
-        x_quantise(0)
-        nc.vector.tensor_copy(out=g1_v[:, 0], in_=mraw_v[:, 0])
-        nc.scalar.copy(out=g1_v[:, 1, 0:3], in_=mraw_v[:, 1, 0:3])
-        m1_quantise(0)
-        nc.vector.tensor_copy(out=g1_v[:, 1, 3:4], in_=mraw_v[:, 1, 3:4])
-        m1_quantise(1)
-        m2_transpose(0, 0, "O")
+        def store(n, cnt):
+            g, i = divmod(n, 4)
+            dview = of[512 * g : 512 * g + 512, :].rearrange("(r i) d -> r i d", i=4)
+            nc.sync.dma_start(
+                out=dview[:, i : i + cnt, :], in_=st["ob%d" % (n // 2)][:, n % 2 : n % 2 + cnt, :]
+            )
+
+        x_transpose(0, 2, "T")
+        x_copy(0, 2, "v")
+        x_quantise(0, 2)
+        m1_regroup(0, "v", 0, 3)
+        m1_regroup(0, "s", 3, 4)
+        m2_transpose(0, 0, "X")
         m2_transpose(0, 1, "O")
+        m1_quantise(0)
+        m2_copy(0, 0, "s")
+        m1_regroup(1, "v", 0, 2)
+        m1_regroup(1, "s", 2, 4)
         m2_transpose(1, 0, "T")
         m2_transpose(1, 1, "T")
-        logits(0)
-        logits(1)
-        for c in range(2):
-            for u in range(2):
-                m2_copy(c, u, "s")
+        m1_quantise(1)
+        logits(0, 0)
+        x_transpose(2, 2, "X")
+        m2_copy(0, 1, "s")
+        x_copy(2, 2, "s")
+        m2_copy(1, 0, "s")
+        m2_copy(1, 1, "s")
+        logits(0, 1)
+        logits(1, 0)
+        logits(1, 1)
 
         def live(n):
             return 0 <= n < NT
 
-        for step in range(NT + 4):
-            if live(step):
-                row_max(step)
-            if step % 2 == 0 and live(step - 1):
-                pair_sum((step - 2) // 2)
-            if step % 2 == 1 and live(step - 2):
-                pair_recip((step - 3) // 2)
-            if live(step):
+        for step in range(NT):
+            last = step == NT - 1
+            row_max(step, 0)
+            row_max(step, 1)
+            if last:
+                neg_bias(step)
+            if live(step - 2):
+                e_copy(step - 2)
+            if not last:
                 neg_bias(step)
             if step == 0:
+                x_quantise(2, 2)
+            if live(step + 3) and step + 3 >= 4:
+                x_quantise(step + 3, 1)
+            if step == 1:
                 m2_quantise(0)
                 m2_quantise(1)
-            if live(step - 1):
-                e_copy(step - 1)
-            if live(step + 3) and step + 3 >= 4:
-                x1_quantise(step + 3)
-            if live(step - 2):
-                e_quantise(step - 2)
-            if live(step - 1):
-                e_regroup(step - 1)
-            if live(step):
-                exp_half(step, 0)
-                e_transpose_half(step, 0)
             if live(step + 4):
-                x1_transpose(step + 4)
-            if live(step):
-                exp_half(step, 1)
-                e_transpose_half(step, 1)
+                x_transpose(step + 4, 1, "X")
             if live(step - 3):
-                out_copy(step - 3)
-            if live(step + 4):
-                x1_copy(step + 4, "s")
+                e_quantise(step - 3)
             if live(step - 2):
-                out_matmul(step - 2)
+                e_regroup(step - 2)
+            exp_half(step, 0)
+            if last:
+                exp_half(step, 1)
+            if step % 2 == 0 and step >= 2:
+                pair_sum((step - 2) // 2)
+            if step % 2 == 1 and step >= 3:
+                pair_recip((step - 3) // 2)
+            if live(step - 1):
+                e_transpose_half(step - 1, 1)
+            e_transpose_half(step, 0)
+            if live(step - 4) and not last:
+                out_copy(step - 4, "s")
+                if (step - 4) % 2 == 1:
+                    store(step - 5, 2)
+            if live(step + 4):
+                x_copy(step + 4, 1, "s")
             if live(step + 2):
-                logits(step + 2)
+                logits(step + 2, 0)
+            if live(step - 3) and not last:
+                out_matmul(step - 3, "O")
+            if not last:
+                exp_half(step, 1)
+            if live(step + 2):
+                logits(step + 2, 1)
+
+        e_copy_short(NT - 2, 0, "v")
+        e_copy_short(NT - 2, 1, "v")
+        e_transpose_half(NT - 1, 1)
+        out_copy(NT - 5, "s")
+        store(NT - 6, 2)
+        out_matmul(NT - 4, "T")
+        e_quantise(NT - 2)
+        e_copy_short(NT - 1, 0, "v")
+        e_copy_short(NT - 1, 1, "s")
+        e_quantise(NT - 3)
+        out_matmul(NT - 2, "T")
+        pair_sum(NT // 2 - 1)
+        e_quantise(NT - 1)
+        pair_recip(NT // 2 - 1)
+        out_matmul(NT - 3, "X")
+        out_matmul(NT - 1, "O")
+        out_copy(NT - 4, "s")
+        store(NT - 4, 1)
+        out_copy(NT - 3, "v")
+        store(NT - 3, 1)
+        out_copy(NT - 2, "s")
+        store(NT - 2, 1)
+        out_copy(NT - 1, "v")
+        store(NT - 1, 1)

@@ -215,9 +215,9 @@ def tile_p4transformerda7_kernel(tc, x, mem, out):
             for t in range(4):
                 nc.tensor.transpose(dst[:, k0 + t, :], e[:, 128 * t : 128 * t + 128], ident_b[:])
 
-        def e_copy(n):
+        def e_copy(n, eng):
             s1 = work.tile([P, M], BF16, name="s1", bufs=2)
-            nc.vector.tensor_copy(out=s1[:], in_=st["tw%d" % n][:].rearrange("q k r -> q (k r)"))
+            copy_on(eng, s1[:], st["tw%d" % n][:].rearrange("q k r -> q (k r)"))
             st["s1_%d" % n] = s1
 
         def e_regroup(n):
@@ -326,8 +326,8 @@ def tile_p4transformerda7_kernel(tc, x, mem, out):
             row_max(step, 1)
             if last:
                 neg_bias(step)
-            if live(step - 2):
-                e_copy(step - 2)
+            if live(step - 2) and step - 2 >= 2:
+                e_copy(step - 2, "v")
             if not last:
                 neg_bias(step)
             if step == 0:
@@ -341,6 +341,8 @@ def tile_p4transformerda7_kernel(tc, x, mem, out):
                 x_transpose(step + 4, 1, "X")
             if live(step - 3):
                 e_quantise(step - 3)
+            if 0 <= step - 2 < 2:
+                e_copy(step - 2, "s")
             if live(step - 2):
                 e_regroup(step - 2)
             exp_half(step, 0)
@@ -373,10 +375,10 @@ def tile_p4transformerda7_kernel(tc, x, mem, out):
         e_transpose_half(NT - 1, 1)
         out_copy(NT - 5, "s")
         store(NT - 6, 2)
-        out_matmul(NT - 4, "T")
-        e_quantise(NT - 2)
         e_copy_short(NT - 1, 0, "v")
         e_copy_short(NT - 1, 1, "s")
+        out_matmul(NT - 4, "T")
+        e_quantise(NT - 2)
         e_quantise(NT - 3)
         out_matmul(NT - 2, "T")
         pair_sum(NT // 2 - 1)
@@ -386,9 +388,9 @@ def tile_p4transformerda7_kernel(tc, x, mem, out):
         out_matmul(NT - 1, "O")
         out_copy(NT - 4, "s")
         store(NT - 4, 1)
-        out_copy(NT - 3, "v")
-        store(NT - 3, 1)
-        out_copy(NT - 2, "s")
+        out_copy(NT - 2, "v")
         store(NT - 2, 1)
+        out_copy(NT - 3, "s")
+        store(NT - 3, 1)
         out_copy(NT - 1, "v")
         store(NT - 1, 1)

from contextlib import ExitStack

import concourse.mybir as mybir
from concourse.masks import make_identity

F32 = mybir.dt.float32
BF16 = mybir.dt.bfloat16
U32 = mybir.dt.uint32
U8 = mybir.dt.uint8
FP8X4 = mybir.dt.float8_e4m3fn_x4
ACT = mybir.ActivationFunctionType
ALU = mybir.AluOpType
AX = mybir.AxisListType

P = 128
D = 512
M = 1024
TOK = 4096
NG = 8
NT = 32
SCALE = 1.0 / (512.0 ** 0.5)
FLOPS = 2 * 2 * TOK * M * D
BANKS = {"L": 4, "T": 2, "X": 1, "O": 1}


def tile_p4transformerda7_kernel(tc, x, mem, out):
    nc = tc.nc
    xf = x.flatten_outer_dims()
    mf = mem.flatten_outer_dims()
    of = out.flatten_outer_dims()

    with ExitStack() as ctx:
        const = ctx.enter_context(tc.tile_pool(name="const", bufs=1))
        work = ctx.enter_context(tc.tile_pool(name="work", bufs=3))
        small = ctx.enter_context(tc.tile_pool(name="small", bufs=6))
        psum = ctx.enter_context(tc.psum_pool(name="psum", bufs=1))
        ctx.enter_context(tc.manual_schedule())

        st = {}

        def bank(shape, dtype, tag, name):
            return psum.tile(shape, dtype, name=name, tag=tag, bufs=BANKS[tag])

        def copy_on(eng, dst, src):
            if eng == "v":
                nc.vector.tensor_copy(out=dst, in_=src)
            else:
                nc.scalar.copy(out=dst, in_=src)

        def x_rows(g):
            return xf[512 * g : 512 * g + 512, :].rearrange("(r i) d -> r i d", i=4)

        def load_x_half(h):
            t = const.tile([P, 2 * D], BF16, name="xs0%d" % h)
            nc.sync.dma_start(
                out=t[:].rearrange("r (i d) -> r i d", i=2), in_=x_rows(0)[:, 2 * h : 2 * h + 2, :]
            )
            for i in range(2):
                st["xw%d" % (2 * h + i)] = t[:].bitcast(F32)[:, 256 * i : 256 * i + 256]

        def load_x(g):
            t = const.tile([P, 4 * D], BF16, name="xs%d" % g)
            nc.sync.dma_start(out=t[:].rearrange("r (i d) -> r i d", i=4), in_=x_rows(g))
            for i in range(4):
                st["xw%d" % (4 * g + i)] = t[:].bitcast(F32)[:, 256 * i : 256 * i + 256]

        mraw = []
        load_x_half(0)
        for c in range(2):
            t = const.tile([P, 4 * 512], BF16, name="mraw%d" % c)
            for u in range(2):
                nc.sync.dma_start(
                    out=t[:].rearrange("q (k j) -> q k j", k=4)[:, 2 * u : 2 * u + 2, :],
                    in_=mf[256 * u : 256 * u + 256, 512 * c : 512 * c + 512].rearrange(
                        "(p e) j -> p e j", e=2
                    ),
                )
            mraw.append(t)
        load_x_half(1)
        for g in range(1, NG):
            load_x(g)

        warm = const.tile([P, 1], F32, name="warm")
        nc.vector.memset(warm[:], 0.0)
        warm2 = const.tile([P, 1], F32, name="warm2")
        nc.scalar.activation(out=warm2[:], in_=warm[:], func=ACT.Exp)
        ident_f = const.tile([P, P], F32, name="ident_f")
        make_identity(nc, ident_f[:])
        ident_b = const.tile([P, P], BF16, name="ident_b")
        make_identity(nc, ident_b[:])

        def x_transpose(n, cnt, tag):
            tx = bank([P, cnt, 2, P], F32, tag, "tx")
            for i in range(cnt):
                for u in range(2):
                    nc.tensor.transpose(
                        tx[:, i, u, :], st["xw%d" % (n + i)][:, 128 * u : 128 * u + 128], ident_f[:]
                    )
            st["tx%d" % n] = tx

        def x_copy(n, cnt, eng):
            gx = work.tile([P, 256 * cnt], F32, name="gx%d" % cnt, align_bytes=64)
            copy_on(
                eng,
                gx[:].rearrange("q (i r u) -> q i r u", i=cnt, r=P, u=2),
                st["tx%d" % n][:].rearrange("q i u r -> q i r u"),
            )
            st["gx%d" % n] = gx

        def x_quantise(n, cnt):
            q = const.tile([P, P * cnt], U32, name="xq%d" % n, align_bytes=64)
            s = const.tile([P, P * cnt], U8, name="xsc%d" % n, align_bytes=64)
            nc.vector.quantize_mx(out=q[:].bitcast(FP8X4), scales=s[:], in_=st["gx%d" % n][:].bitcast(BF16))
            for i in range(cnt):
                st["xc%d" % (n + i)] = (q[:, 128 * i : 128 * i + 128], s[:, 128 * i : 128 * i + 128])

        def m1_regroup(c, eng, t0, t1):
            if ("g1_%d" % c) not in st:
                g1 = const.tile([P, 2048], BF16, name="g1_%d" % c, align_bytes=64)
                st["g1_%d" % c] = g1
            dst = st["g1_%d" % c][:].rearrange("q (t p k) -> q t p k", t=4, p=P, k=4)
            src = mraw[c][:].rearrange("q (k p t) -> q t p k", k=4, p=P, t=4)
            copy_on(eng, dst[:, t0:t1], src[:, t0:t1])

        def m1_quantise(c):
            q = const.tile([P, 512], U32, name="m1q%d" % c, align_bytes=64)
            s = const.tile([P, 512], U8, name="m1s%d" % c, align_bytes=64)
            nc.vector.quantize_mx(out=q[:].bitcast(FP8X4), scales=s[:], in_=st["g1_%d" % c][:])
            st["m1_%d" % c] = (q, s)

        def m2_transpose(c, u, tag):
            mw = mraw[c][:].bitcast(F32).rearrange("q (k w) -> q k w", k=4)
            tm = bank([P, 2, 2, P], F32, tag, "tm")
            for e in range(2):
                for v in range(2):
                    nc.tensor.transpose(tm[:, e, v, :], mw[:, 2 * u + e, v : 256 : 2], ident_f[:])
            st["tm%d%d" % (c, u)] = tm

        def m2_copy(c, u, eng):
            if ("g2_%d" % c) not in st:
                g2 = const.tile([P, 1024], F32, name="g2_%d" % c, align_bytes=64)
                st["g2_%d" % c] = g2
            dst = st["g2_%d" % c][:].rearrange("q (u a e v) -> q u a e v", u=2, a=P, e=2, v=2)
            copy_on(eng, dst[:, u], st["tm%d%d" % (c, u)][:].rearrange("q e v a -> q a e v"))

        def m2_quantise(c):
            q = const.tile([P, 512], U32, name="m2q%d" % c, align_bytes=64)
            s = const.tile([P, 512], U8, name="m2s%d" % c, align_bytes=64)
            nc.vector.quantize_mx(out=q[:].bitcast(FP8X4), scales=s[:], in_=st["g2_%d" % c][:].bitcast(BF16))
            st["m2_%d" % c] = (q, s)

        def logits(n, c):
            codes, scales = st["xc%d" % n]
            q, s = st["m1_%d" % c]
            lg = bank([P, 512], F32, "L", "lg")
            nc.tensor.matmul_mx(
                out=lg[:],
                lhsT=codes.bitcast(FP8X4),
                lhsT_scale=scales,
                rhs=q[:].bitcast(FP8X4),
                rhs_scale=s[:],
                start=True,
                stop=True,
            )
            st["lg%d_%d" % (n, c)] = lg

        def row_max(n, c):
            if c == 0:
                mx = small.tile([P, 2], F32, name="mx")
                st["mx%d" % n] = mx
            nc.vector.reduce_max(
                out=st["mx%d" % n][:, c : c + 1], in_=st["lg%d_%d" % (n, c)][:], axis=AX.X
            )

        def neg_bias(n):
            mx = st["mx%d" % n]
            nb = small.tile([P, 1], F32, name="nb")
            nc.vector.tensor_scalar(
                out=nb[:], in0=mx[:, 0:1], scalar1=mx[:, 1:2], scalar2=-SCALE, op0=ALU.max, op1=ALU.mult
            )
            st["nb%d" % n] = nb

        def exp_half(n, c):
            if n % 2 == 0 and c == 0:
                ss = small.tile([P, 2, 2], F32, name="ss")
                st["ss%d" % (n // 2)] = ss
            ss = st["ss%d" % (n // 2)]
            e = work.tile([P, 512], BF16, name="e%d" % c)
            nc.scalar.activation(
                out=e[:],
                in_=st["lg%d_%d" % (n, c)][:],
                func=ACT.Exp,
                bias=st["nb%d" % n][:],
                scale=SCALE,
                accum_out=ss[:, n % 2, c : c + 1],
            )
            st["e%d_%d" % (n, c)] = e

        def short_way(n):
            return n >= NT - 2

        def e_transpose_half(n, c):
            e = st["e%d_%d" % (n, c)]
            if short_way(n):
                td = bank([P, 4, P], BF16, "L", "td")
                st["td%d_%d" % (n, c)] = td
                dst = td
                k0 = 0
            else:
                if c == 0:
                    tw = bank([P, 8, P], BF16, "T", "tw")
                    st["tw%d" % n] = tw
                dst = st["tw%d" % n]
                k0 = 4 * c
            for t in range(4):
                nc.tensor.transpose(dst[:, k0 + t, :], e[:, 128 * t : 128 * t + 128], ident_b[:])

        def e_copy(n, eng):
            s1 = work.tile([P, M], BF16, name="s1", bufs=2)
            copy_on(eng, s1[:], st["tw%d" % n][:].rearrange("q k r -> q (k r)"))
            st["s1_%d" % n] = s1

        def e_regroup(n):
            ge = work.tile([P, M], BF16, name="ge", align_bytes=64, bufs=2)
            nc.gpsimd.tensor_scalar(
                out=ge[:].rearrange("q (c r t) -> q c r t", c=2, r=P, t=4),
                in0=st["s1_%d" % n][:].rearrange("q (c t r) -> q c r t", c=2, t=4, r=P),
                scalar1=1.0,
                scalar2=0.0,
                op0=ALU.mult,
                op1=ALU.add,
            )
            st["ge%d" % n] = ge

        def e_copy_short(n, c, eng):
            if ("ge%d" % n) not in st:
                ge = work.tile([P, M], BF16, name="ged", align_bytes=64, bufs=2)
                st["ge%d" % n] = ge
            dst = st["ge%d" % n][:].rearrange("q (c r t) -> q c r t", c=2, r=P, t=4)
            copy_on(eng, dst[:, c], st["td%d_%d" % (n, c)][:].rearrange("q t r -> q r t"))

        def e_quantise(n):
            eq = work.tile([P, 256], U32, name="eq", align_bytes=64, bufs=4)
            es = work.tile([P, 256], U8, name="es", align_bytes=64, bufs=4)
            nc.vector.quantize_mx(out=eq[:].bitcast(FP8X4), scales=es[:], in_=st["ge%d" % n][:])
            st["eq%d" % n] = eq
            st["es%d" % n] = es

        def pair_sum(pr):
            tot = small.tile([P, 2], F32, name="tot")
            nc.vector.reduce_sum(out=tot[:], in_=st["ss%d" % pr][:], axis=AX.X)
            st["tot%d" % pr] = tot

        def pair_recip(pr):
            rc = small.tile([P, 2], F32, name="rc")
            nc.vector.reciprocal(out=rc[:], in_=st["tot%d" % pr][:])
            st["rc%d" % pr] = rc

        def out_matmul(n, tag):
            eq = st["eq%d" % n]
            es = st["es%d" % n]
            acc = bank([P, D], F32, tag, "acc")
            for c in range(2):
                q, s = st["m2_%d" % c]
                nc.tensor.matmul_mx(
                    out=acc[:],
                    lhsT=eq[:, 128 * c : 128 * c + 128].bitcast(FP8X4),
                    lhsT_scale=es[:, 128 * c : 128 * c + 128],
                    rhs=q[:].bitcast(FP8X4),
                    rhs_scale=s[:],
                    start=(c == 0),
                    stop=(c == 1),
                )
            st["acc%d" % n] = acc

        def out_copy(n, eng):
            if n % 2 == 0:
                ob = work.tile([P, 2, D], F32, name="ob")
                st["ob%d" % (n // 2)] = ob
            ob = st["ob%d" % (n // 2)]
            rc = st["rc%d" % (n // 2)][:, n % 2 : n % 2 + 1]
            if eng == "v":
                nc.vector.tensor_scalar(
                    out=ob[:, n % 2, :], in0=st["acc%d" % n][:], scalar1=rc, scalar2=None, op0=ALU.mult
                )
            else:
                nc.scalar.activation(out=ob[:, n % 2, :], in_=st["acc%d" % n][:], func=ACT.Copy, scale=rc)

        def store(n, cnt):
            g, i = divmod(n, 4)
            dview = of[512 * g : 512 * g + 512, :].rearrange("(r i) d -> r i d", i=4)
            nc.sync.dma_start(
                out=dview[:, i : i + cnt, :], in_=st["ob%d" % (n // 2)][:, n % 2 : n % 2 + cnt, :]
            )

        x_transpose(0, 2, "T")
        x_copy(0, 2, "v")
        x_quantise(0, 2)
        m1_regroup(0, "v", 0, 3)
        m1_regroup(0, "s", 3, 4)
        m2_transpose(0, 0, "X")
        m2_transpose(0, 1, "O")
        m1_quantise(0)
        m2_copy(0, 0, "s")
        m1_regroup(1, "v", 0, 2)
        m1_regroup(1, "s", 2, 4)
        m2_transpose(1, 0, "T")
        m2_transpose(1, 1, "T")
        m1_quantise(1)
        logits(0, 0)
        x_transpose(2, 2, "X")
        m2_copy(0, 1, "s")
        x_copy(2, 2, "s")
        m2_copy(1, 0, "s")
        m2_copy(1, 1, "s")
        logits(0, 1)
        logits(1, 0)
        logits(1, 1)

        def live(n):
            return 0 <= n < NT

        for step in range(NT):
            last = step == NT - 1
            row_max(step, 0)
            row_max(step, 1)
            if last:
                neg_bias(step)
            if live(step - 2) and step - 2 >= 2:
                e_copy(step - 2, "v")
            if not last:
                neg_bias(step)
            if step == 0:
                x_quantise(2, 2)
            if live(step + 3) and step + 3 >= 4:
                x_quantise(step + 3, 1)
            if step == 1:
                m2_quantise(0)
                m2_quantise(1)
            if live(step + 4):
                x_transpose(step + 4, 1, "X")
            if live(step - 3):
                e_quantise(step - 3)
            if 0 <= step - 2 < 2:
                e_copy(step - 2, "s")
            if live(step - 2):
                e_regroup(step - 2)
            exp_half(step, 0)
            if last:
                exp_half(step, 1)
            if step % 2 == 0 and step >= 2:
                pair_sum((step - 2) // 2)
            if step % 2 == 1 and step >= 3:
                pair_recip((step - 3) // 2)
            if live(step - 1):
                e_transpose_half(step - 1, 1)
            e_transpose_half(step, 0)
            if live(step - 4) and not last:
                out_copy(step - 4, "s")
                if (step - 4) % 2 == 1:
                    store(step - 5, 2)
            if live(step + 4):
                x_copy(step + 4, 1, "s")
            if live(step + 2):
                logits(step + 2, 0)
            if live(step - 3) and not last:
                out_matmul(step - 3, "O")
            if not last:
                exp_half(step, 1)
            if live(step + 2):
                logits(step + 2, 1)

        e_copy_short(NT - 2, 0, "v")
        e_copy_short(NT - 2, 1, "v")
        e_transpose_half(NT - 1, 1)
        out_copy(NT - 5, "s")
        store(NT - 6, 2)
        e_copy_short(NT - 1, 0, "v")
        e_copy_short(NT - 1, 1, "s")
        out_matmul(NT - 4, "T")
        e_quantise(NT - 2)
        e_quantise(NT - 3)
        out_matmul(NT - 2, "T")
        pair_sum(NT // 2 - 1)
        e_quantise(NT - 1)
        pair_recip(NT // 2 - 1)
        out_matmul(NT - 3, "X")
        out_matmul(NT - 1, "O")
        out_copy(NT - 4, "s")
        store(NT - 4, 1)
        out_copy(NT - 2, "v")
        store(NT - 2, 1)
        out_copy(NT - 3, "s")
        store(NT - 3, 1)
        out_copy(NT - 1, "v")
        store(NT - 1, 1)
